import numpy as np
import ml_dtypes

BF16 = ml_dtypes.bfloat16


def bf(x):
    return np.asarray(x, np.float32).astype(BF16)


def f32(x):
    return np.asarray(x, np.float32)


def f64(x):
    return np.asarray(x).astype(np.float64)


def striped(idx):
    return np.tile(idx.reshape(-1, 16).T, (8, 1))


C, S, N, BIN, KP = 256, 1024, 2048, 2, 2


def bin_softmax(v):
    e = np.exp(v).reshape(C, S // BIN, BIN)
    return (e / e.sum(axis=-1, keepdims=True)).reshape(C, S)


def setup_inputs():
    logits = f32(np.random.standard_normal((1, S)) + np.random.uniform(-1.0, 1.0, (C, S)))
    idx = np.concatenate([np.random.permutation(S) for _ in range(KP)])
    return {"logits": logits, "offs": striped(idx)}


def reference(logits, offs):
    idx = offs[:16].T.reshape(-1)
    p = bin_softmax(f64(logits))
    t = p.copy()
    for k in range(KP):
        t = t * p[:, idx[k * S:(k + 1) * S]]
    return t.mean(axis=0, keepdims=True)

@@ -1,0 +1,68 @@
+import concourse.mybir as mybir
+
+F32 = mybir.dt.float32
+BF16 = mybir.dt.bfloat16
+U16 = mybir.dt.uint16
+MULT = mybir.AluOpType.mult
+SUBTRACT = mybir.AluOpType.subtract
+SIGMOID = mybir.ActivationFunctionType.Sigmoid
+
+P = 128
+RECORDS = 256
+COLUMNS = 1024
+PAIRS = COLUMNS // 2
+BLOCKS = RECORDS // P
+LOOKUPS = 2
+BANK = 512
+BANKS = COLUMNS // BANK
+LIST_COLUMNS = COLUMNS // 16
+
+FLOPS = 2 * RECORDS * COLUMNS
+
+
+def tile_rap_kernel(tc, logits, offs, out):
+    nc = tc.nc
+    with (
+        tc.tile_pool(name="held", bufs=1) as held,
+        tc.psum_pool(name="psum", bufs=1) as psum,
+    ):
+        offsets = held.tile([P, LOOKUPS * LIST_COLUMNS], U16, name="offsets")
+        nc.sync.dma_start(offsets[:], offs)
+
+        averager = held.tile([P, 1], BF16, name="averager")
+        nc.vector.memset(averager[:], 1.0 / RECORDS)
+
+        sums = [psum.tile([1, BANK], F32, name=f"sums{h}") for h in range(BANKS)]
+
+        for b in range(BLOCKS):
+            raw = held.tile([P, COLUMNS], F32, name=f"raw{b}")
+            nc.sync.dma_start(raw[:], logits[b * P : (b + 1) * P, :])
+
+            halves = raw[:].rearrange("p (a two) -> p two a", two=2)
+            margins = held.tile([P, COLUMNS], F32, name=f"margins{b}")
+            nc.vector.tensor_tensor(margins[:, 0:PAIRS], halves[:, 0, :], halves[:, 1, :], SUBTRACT)
+            nc.vector.tensor_scalar_mul(margins[:, PAIRS:COLUMNS], margins[:, 0:PAIRS], -1.0)
+
+            in_order = margins[:].rearrange("p (two a) -> p a two", two=2)
+            window = held.tile([P, COLUMNS], F32, name=f"window{b}")
+            own = held.tile([P, COLUMNS], F32, name=f"own{b}")
+            for p_tile in (window, own):
+                nc.scalar.activation(p_tile[:].rearrange("p (a two) -> p a two", two=2), in_order, SIGMOID)
+
+            product = own
+            for k in range(LOOKUPS):
+                picked = window[:].indirect(offsets[:, k * LIST_COLUMNS : (k + 1) * LIST_COLUMNS])
+                longer = held.tile([P, COLUMNS], F32, name=f"product{b}_{k}")
+                nc.vector.tensor_tensor(longer[:], picked, product[:], MULT)
+                product = longer
+
+            rounded = held.tile([P, COLUMNS], BF16, name=f"rounded{b}")
+            for h in range(BANKS):
+                bank = slice(h * BANK, (h + 1) * BANK)
+                nc.scalar.copy(rounded[:, bank], product[:, bank])
+                nc.tensor.matmul(sums[h][:], averager[:], rounded[:, bank], start=(b == 0), stop=(b == BLOCKS - 1))
+
+        answers = held.tile([1, COLUMNS], F32, name="answers")
+        for h in range(BANKS):
+            nc.scalar.copy(answers[:, h * BANK : (h + 1) * BANK], sums[h][:])
+        nc.sync.dma_start(out, answers[:])

@@ -9,60 +9,69 @@ SIGMOID = mybir.ActivationFunctionType.Sigmoid
 
 P = 128
 RECORDS = 256
-COLUMNS = 1024
-PAIRS = COLUMNS // 2
 BLOCKS = RECORDS // P
+COLUMNS = 1024
 LOOKUPS = 2
-BANK = 512
-BANKS = COLUMNS // BANK
-LIST_COLUMNS = COLUMNS // 16
+PIECE = 512
+PIECES = COLUMNS // PIECE
+PAIRS = PIECE // 2
 
 FLOPS = 2 * RECORDS * COLUMNS
 
 
 def tile_rap_kernel(tc, logits, offs, out):
     nc = tc.nc
+    pieces = [slice(h * PIECE, (h + 1) * PIECE) for h in range(PIECES)]
     with (
         tc.tile_pool(name="held", bufs=1) as held,
         tc.psum_pool(name="psum", bufs=1) as psum,
     ):
-        offsets = held.tile([P, LOOKUPS * LIST_COLUMNS], U16, name="offsets")
+        offsets = held.tile([P, LOOKUPS * COLUMNS // 16], U16, name="offsets")
         nc.sync.dma_start(offsets[:], offs)
+
+        raw = [held.tile([P, COLUMNS], F32, name=f"raw{b}") for b in range(BLOCKS)]
+        for b in range(BLOCKS):
+            for piece in pieces:
+                nc.sync.dma_start(raw[b][:, piece], logits[b * P : (b + 1) * P, piece])
 
         averager = held.tile([P, 1], BF16, name="averager")
         nc.vector.memset(averager[:], 1.0 / RECORDS)
 
-        sums = [psum.tile([1, BANK], F32, name=f"sums{h}") for h in range(BANKS)]
-
+        window = [held.tile([P, COLUMNS], F32, name=f"window{b}") for b in range(BLOCKS)]
+        own = [held.tile([P, COLUMNS], F32, name=f"own{b}") for b in range(BLOCKS)]
         for b in range(BLOCKS):
-            raw = held.tile([P, COLUMNS], F32, name=f"raw{b}")
-            nc.sync.dma_start(raw[:], logits[b * P : (b + 1) * P, :])
-
-            halves = raw[:].rearrange("p (a two) -> p two a", two=2)
             margins = held.tile([P, COLUMNS], F32, name=f"margins{b}")
-            nc.vector.tensor_tensor(margins[:, 0:PAIRS], halves[:, 0, :], halves[:, 1, :], SUBTRACT)
-            nc.vector.tensor_scalar_mul(margins[:, PAIRS:COLUMNS], margins[:, 0:PAIRS], -1.0)
+            for piece in pieces:
+                sides = raw[b][:, piece].rearrange("p (a two) -> p two a", two=2)
+                differences = margins[:, piece][:, 0:PAIRS]
+                negatives = margins[:, piece][:, PAIRS:PIECE]
+                nc.vector.tensor_tensor(differences, sides[:, 0, :], sides[:, 1, :], SUBTRACT)
+                nc.vector.tensor_scalar_mul(negatives, differences, -1.0)
+            for p_tile in (window[b], own[b]):
+                for piece in pieces:
+                    nc.scalar.activation(
+                        p_tile[:, piece].rearrange("p (a two) -> p a two", two=2),
+                        margins[:, piece].rearrange("p (two a) -> p a two", two=2),
+                        SIGMOID,
+                    )
 
-            in_order = margins[:].rearrange("p (two a) -> p a two", two=2)
-            window = held.tile([P, COLUMNS], F32, name=f"window{b}")
-            own = held.tile([P, COLUMNS], F32, name=f"own{b}")
-            for p_tile in (window, own):
-                nc.scalar.activation(p_tile[:].rearrange("p (a two) -> p a two", two=2), in_order, SIGMOID)
-
-            product = own
+        sums = [psum.tile([1, PIECE], F32, name=f"sums{h}") for h in range(PIECES)]
+        for b in range(BLOCKS):
+            product = own[b]
             for k in range(LOOKUPS):
-                picked = window[:].indirect(offsets[:, k * LIST_COLUMNS : (k + 1) * LIST_COLUMNS])
                 longer = held.tile([P, COLUMNS], F32, name=f"product{b}_{k}")
-                nc.vector.tensor_tensor(longer[:], picked, product[:], MULT)
+                for h, piece in enumerate(pieces):
+                    first = (k * COLUMNS + h * PIECE) // 16
+                    picked = window[b][:].indirect(offsets[:, first : first + PIECE // 16])
+                    nc.vector.tensor_tensor(longer[:, piece], picked, product[:, piece], MULT)
                 product = longer
 
             rounded = held.tile([P, COLUMNS], BF16, name=f"rounded{b}")
-            for h in range(BANKS):
-                bank = slice(h * BANK, (h + 1) * BANK)
-                nc.scalar.copy(rounded[:, bank], product[:, bank])
-                nc.tensor.matmul(sums[h][:], averager[:], rounded[:, bank], start=(b == 0), stop=(b == BLOCKS - 1))
+            for h, piece in enumerate(pieces):
+                nc.scalar.copy(rounded[:, piece], product[:, piece])
+                nc.tensor.matmul(sums[h][:], averager[:], rounded[:, piece], start=(b == 0), stop=(b == BLOCKS - 1))
 
         answers = held.tile([1, COLUMNS], F32, name="answers")
-        for h in range(BANKS):
-            nc.scalar.copy(answers[:, h * BANK : (h + 1) * BANK], sums[h][:])
-        nc.sync.dma_start(out, answers[:])
+        for h, piece in enumerate(pieces):
+            nc.scalar.copy(answers[:, piece], sums[h][:])
+            nc.sync.dma_start(out[:, piece], answers[:, piece])

@@ -11,17 +11,16 @@ P = 128
 RECORDS = 256
 BLOCKS = RECORDS // P
 COLUMNS = 1024
+PAIRS = COLUMNS // 2
 LOOKUPS = 2
-PIECE = 512
-PIECES = COLUMNS // PIECE
-PAIRS = PIECE // 2
+LOAD = 512
+PIECE = 256
 
 FLOPS = 2 * RECORDS * COLUMNS
 
 
 def tile_rap_kernel(tc, logits, offs, out):
     nc = tc.nc
-    pieces = [slice(h * PIECE, (h + 1) * PIECE) for h in range(PIECES)]
     with (
         tc.tile_pool(name="held", bufs=1) as held,
         tc.psum_pool(name="psum", bufs=1) as psum,
@@ -31,47 +30,53 @@ def tile_rap_kernel(tc, logits, offs, out):
 
         raw = [held.tile([P, COLUMNS], F32, name=f"raw{b}") for b in range(BLOCKS)]
         for b in range(BLOCKS):
-            for piece in pieces:
-                nc.sync.dma_start(raw[b][:, piece], logits[b * P : (b + 1) * P, piece])
+            for queue, c in zip((nc.sync, nc.scalar), range(0, COLUMNS, LOAD)):
+                queue.dma_start(raw[b][:, c : c + LOAD], logits[b * P : (b + 1) * P, c : c + LOAD])
 
         averager = held.tile([P, 1], BF16, name="averager")
         nc.vector.memset(averager[:], 1.0 / RECORDS)
 
+        scratch = held.tile([P, 1], F32, name="scratch")
+        nc.vector.memset(scratch[:], 0.0)
+        warmed = held.tile([P, 1], F32, name="warmed")
+        nc.scalar.activation(warmed[:], scratch[:], SIGMOID)
+
         window = [held.tile([P, COLUMNS], F32, name=f"window{b}") for b in range(BLOCKS)]
         own = [held.tile([P, COLUMNS], F32, name=f"own{b}") for b in range(BLOCKS)]
         for b in range(BLOCKS):
-            margins = held.tile([P, COLUMNS], F32, name=f"margins{b}")
-            for piece in pieces:
-                sides = raw[b][:, piece].rearrange("p (a two) -> p two a", two=2)
-                differences = margins[:, piece][:, 0:PAIRS]
-                negatives = margins[:, piece][:, PAIRS:PIECE]
-                nc.vector.tensor_tensor(differences, sides[:, 0, :], sides[:, 1, :], SUBTRACT)
-                nc.vector.tensor_scalar_mul(negatives, differences, -1.0)
+            sides = raw[b][:].rearrange("p (a two) -> p two a", two=2)
+            margins = held.tile([P, 2 * PAIRS], F32, name=f"margins{b}")
+            differences = margins[:, 0:PAIRS]
+            negatives = margins[:, PAIRS : 2 * PAIRS]
+            for a in range(0, PAIRS, LOAD // 2):
+                pairs = slice(a, a + LOAD // 2)
+                nc.vector.tensor_tensor(differences[:, pairs], sides[:, 0, pairs], sides[:, 1, pairs], SUBTRACT)
+                nc.vector.tensor_scalar_mul(negatives[:, pairs], differences[:, pairs], -1.0)
+            in_order = margins[:].rearrange("p (two a) -> p a two", two=2)
             for p_tile in (window[b], own[b]):
-                for piece in pieces:
-                    nc.scalar.activation(
-                        p_tile[:, piece].rearrange("p (a two) -> p a two", two=2),
-                        margins[:, piece].rearrange("p (two a) -> p a two", two=2),
-                        SIGMOID,
-                    )
+                p_pairs = p_tile[:].rearrange("p (a two) -> p a two", two=2)
+                for a in range(0, PAIRS, PIECE // 2):
+                    pairs = slice(a, a + PIECE // 2)
+                    nc.scalar.activation(p_pairs[:, pairs, :], in_order[:, pairs, :], SIGMOID)
 
-        sums = [psum.tile([1, PIECE], F32, name=f"sums{h}") for h in range(PIECES)]
+        starts = range(0, COLUMNS, PIECE)
+        sums = [psum.tile([1, PIECE], F32, name=f"sums{j}") for j in starts]
         for b in range(BLOCKS):
             product = own[b]
             for k in range(LOOKUPS):
                 longer = held.tile([P, COLUMNS], F32, name=f"product{b}_{k}")
-                for h, piece in enumerate(pieces):
-                    first = (k * COLUMNS + h * PIECE) // 16
+                for j in starts:
+                    first = (k * COLUMNS + j) // 16
                     picked = window[b][:].indirect(offsets[:, first : first + PIECE // 16])
-                    nc.vector.tensor_tensor(longer[:, piece], picked, product[:, piece], MULT)
+                    nc.vector.tensor_tensor(longer[:, j : j + PIECE], picked, product[:, j : j + PIECE], MULT)
                 product = longer
 
             rounded = held.tile([P, COLUMNS], BF16, name=f"rounded{b}")
-            for h, piece in enumerate(pieces):
-                nc.scalar.copy(rounded[:, piece], product[:, piece])
-                nc.tensor.matmul(sums[h][:], averager[:], rounded[:, piece], start=(b == 0), stop=(b == BLOCKS - 1))
+            for bank, j in zip(sums, starts):
+                nc.scalar.copy(rounded[:, j : j + PIECE], product[:, j : j + PIECE])
+                nc.tensor.matmul(bank[:], averager[:], rounded[:, j : j + PIECE], start=(b == 0), stop=(b == BLOCKS - 1))
 
         answers = held.tile([1, COLUMNS], F32, name="answers")
-        for h, piece in enumerate(pieces):
-            nc.scalar.copy(answers[:, piece], sums[h][:])
-            nc.sync.dma_start(out[:, piece], answers[:, piece])
+        for bank, j in zip(sums, starts):
+            nc.scalar.copy(answers[:, j : j + PIECE], bank[:])
+            nc.sync.dma_start(out[:, j : j + PIECE], answers[:, j : j + PIECE])

@@ -13,7 +13,6 @@ BLOCKS = RECORDS // P
 COLUMNS = 1024
 PAIRS = COLUMNS // 2
 LOOKUPS = 2
-LOAD = 512
 PIECE = 256
 
 FLOPS = 2 * RECORDS * COLUMNS
@@ -29,9 +28,11 @@ def tile_rap_kernel(tc, logits, offs, out):
         nc.sync.dma_start(offsets[:], offs)
 
         raw = [held.tile([P, COLUMNS], F32, name=f"raw{b}") for b in range(BLOCKS)]
+        queues = (nc.sync, nc.scalar)
         for b in range(BLOCKS):
-            for queue, c in zip((nc.sync, nc.scalar), range(0, COLUMNS, LOAD)):
-                queue.dma_start(raw[b][:, c : c + LOAD], logits[b * P : (b + 1) * P, c : c + LOAD])
+            for j in range(0, COLUMNS, PIECE):
+                queue = queues[(j // PIECE) % len(queues)]
+                queue.dma_start(raw[b][:, j : j + PIECE], logits[b * P : (b + 1) * P, j : j + PIECE])
 
         averager = held.tile([P, 1], BF16, name="averager")
         nc.vector.memset(averager[:], 1.0 / RECORDS)
@@ -48,8 +49,8 @@ def tile_rap_kernel(tc, logits, offs, out):
             margins = held.tile([P, 2 * PAIRS], F32, name=f"margins{b}")
             differences = margins[:, 0:PAIRS]
             negatives = margins[:, PAIRS : 2 * PAIRS]
-            for a in range(0, PAIRS, LOAD // 2):
-                pairs = slice(a, a + LOAD // 2)
+            for a in range(0, PAIRS, PIECE // 2):
+                pairs = slice(a, a + PIECE // 2)
                 nc.vector.tensor_tensor(differences[:, pairs], sides[:, 0, pairs], sides[:, 1, pairs], SUBTRACT)
                 nc.vector.tensor_scalar_mul(negatives[:, pairs], differences[:, pairs], -1.0)
             in_order = margins[:].rearrange("p (two a) -> p a two", two=2)

@@ -25,7 +25,6 @@ def tile_rap_kernel(tc, logits, offs, out):
         tc.psum_pool(name="psum", bufs=1) as psum,
     ):
         offsets = held.tile([P, LOOKUPS * COLUMNS // 16], U16, name="offsets")
-        nc.sync.dma_start(offsets[:], offs)
 
         raw = [held.tile([P, COLUMNS], F32, name=f"raw{b}") for b in range(BLOCKS)]
         queues = (nc.sync, nc.scalar)
@@ -33,6 +32,8 @@ def tile_rap_kernel(tc, logits, offs, out):
             for j in range(0, COLUMNS, PIECE):
                 queue = queues[(j // PIECE) % len(queues)]
                 queue.dma_start(raw[b][:, j : j + PIECE], logits[b * P : (b + 1) * P, j : j + PIECE])
+            if b == 0:
+                nc.sync.dma_start(offsets[:], offs)
 
         averager = held.tile([P, 1], BF16, name="averager")
         nc.vector.memset(averager[:], 1.0 / RECORDS)
@@ -74,10 +75,16 @@ def tile_rap_kernel(tc, logits, offs, out):
 
             rounded = held.tile([P, COLUMNS], BF16, name=f"rounded{b}")
             for bank, j in zip(sums, starts):
-                nc.scalar.copy(rounded[:, j : j + PIECE], product[:, j : j + PIECE])
+                if b == BLOCKS - 1 and j == starts[-1]:
+                    nc.vector.tensor_copy(rounded[:, j : j + PIECE], product[:, j : j + PIECE])
+                else:
+                    nc.scalar.copy(rounded[:, j : j + PIECE], product[:, j : j + PIECE])
                 nc.tensor.matmul(bank[:], averager[:], rounded[:, j : j + PIECE], start=(b == 0), stop=(b == BLOCKS - 1))
 
         answers = held.tile([1, COLUMNS], F32, name="answers")
         for bank, j in zip(sums, starts):
-            nc.scalar.copy(answers[:, j : j + PIECE], bank[:])
+            if j == starts[-1]:
+                nc.vector.tensor_copy(answers[:, j : j + PIECE], bank[:])
+            else:
+                nc.scalar.copy(answers[:, j : j + PIECE], bank[:])
             nc.sync.dma_start(out[:, j : j + PIECE], answers[:, j : j + PIECE])

@@ -28,12 +28,13 @@ def tile_rap_kernel(tc, logits, offs, out):
 
         raw = [held.tile([P, COLUMNS], F32, name=f"raw{b}") for b in range(BLOCKS)]
         queues = (nc.sync, nc.scalar)
-        for b in range(BLOCKS):
-            for j in range(0, COLUMNS, PIECE):
-                queue = queues[(j // PIECE) % len(queues)]
-                queue.dma_start(raw[b][:, j : j + PIECE], logits[b * P : (b + 1) * P, j : j + PIECE])
-            if b == 0:
-                nc.sync.dma_start(offsets[:], offs)
+        for j in range(0, COLUMNS, PIECE):
+            queue = queues[(j // PIECE) % len(queues)]
+            queue.dma_start(raw[0][:, j : j + PIECE], logits[0:P, j : j + PIECE])
+        nc.sync.dma_start(offsets[:], offs)
+        for b in range(1, BLOCKS):
+            for j in range(0, COLUMNS, COLUMNS // 2):
+                nc.sync.dma_start(raw[b][:, j : j + COLUMNS // 2], logits[b * P : (b + 1) * P, j : j + COLUMNS // 2])
 
         averager = held.tile([P, 1], BF16, name="averager")
         nc.vector.memset(averager[:], 1.0 / RECORDS)
@@ -53,7 +54,10 @@ def tile_rap_kernel(tc, logits, offs, out):
             for a in range(0, PAIRS, PIECE // 2):
                 pairs = slice(a, a + PIECE // 2)
                 nc.vector.tensor_tensor(differences[:, pairs], sides[:, 0, pairs], sides[:, 1, pairs], SUBTRACT)
-                nc.vector.tensor_scalar_mul(negatives[:, pairs], differences[:, pairs], -1.0)
+                if b == 0:
+                    nc.vector.tensor_scalar_mul(negatives[:, pairs], differences[:, pairs], -1.0)
+                else:
+                    nc.scalar.mul(negatives[:, pairs], differences[:, pairs], -1.0)
             in_order = margins[:].rearrange("p (two a) -> p a two", two=2)
             for p_tile in (window[b], own[b]):
                 p_pairs = p_tile[:].rearrange("p (a two) -> p a two", two=2)
@@ -67,10 +71,12 @@ def tile_rap_kernel(tc, logits, offs, out):
             product = own[b]
             for k in range(LOOKUPS):
                 longer = held.tile([P, COLUMNS], F32, name=f"product{b}_{k}")
-                for j in starts:
+                at_an_end = (b, k) in ((0, 0), (BLOCKS - 1, LOOKUPS - 1))
+                width = PIECE if at_an_end else 2 * PIECE
+                for j in range(0, COLUMNS, width):
                     first = (k * COLUMNS + j) // 16
-                    picked = window[b][:].indirect(offsets[:, first : first + PIECE // 16])
-                    nc.vector.tensor_tensor(longer[:, j : j + PIECE], picked, product[:, j : j + PIECE], MULT)
+                    picked = window[b][:].indirect(offsets[:, first : first + width // 16])
+                    nc.vector.tensor_tensor(longer[:, j : j + width], picked, product[:, j : j + width], MULT)
                 product = longer
 
             rounded = held.tile([P, COLUMNS], BF16, name=f"rounded{b}")

@@ -51,8 +51,9 @@ def tile_rap_kernel(tc, logits, offs, out):
             margins = held.tile([P, 2 * PAIRS], F32, name=f"margins{b}")
             differences = margins[:, 0:PAIRS]
             negatives = margins[:, PAIRS : 2 * PAIRS]
-            for a in range(0, PAIRS, PIECE // 2):
-                pairs = slice(a, a + PIECE // 2)
+            step = PIECE // 2 if b == 0 else PAIRS // 2
+            for a in range(0, PAIRS, step):
+                pairs = slice(a, a + step)
                 nc.vector.tensor_tensor(differences[:, pairs], sides[:, 0, pairs], sides[:, 1, pairs], SUBTRACT)
                 if b == 0:
                     nc.vector.tensor_scalar_mul(negatives[:, pairs], differences[:, pairs], -1.0)
@@ -61,8 +62,8 @@ def tile_rap_kernel(tc, logits, offs, out):
             in_order = margins[:].rearrange("p (two a) -> p a two", two=2)
             for p_tile in (window[b], own[b]):
                 p_pairs = p_tile[:].rearrange("p (a two) -> p a two", two=2)
-                for a in range(0, PAIRS, PIECE // 2):
-                    pairs = slice(a, a + PIECE // 2)
+                for a in range(0, PAIRS, step):
+                    pairs = slice(a, a + step)
                     nc.scalar.activation(p_pairs[:, pairs, :], in_order[:, pairs, :], SIGMOID)
 
         starts = range(0, COLUMNS, PIECE)

@@ -47,19 +47,23 @@ def tile_rap_kernel(tc, logits, offs, out):
         window = [held.tile([P, COLUMNS], F32, name=f"window{b}") for b in range(BLOCKS)]
         own = [held.tile([P, COLUMNS], F32, name=f"own{b}") for b in range(BLOCKS)]
         for b in range(BLOCKS):
-            sides = raw[b][:].rearrange("p (a two) -> p two a", two=2)
-            margins = held.tile([P, 2 * PAIRS], F32, name=f"margins{b}")
-            differences = margins[:, 0:PAIRS]
-            negatives = margins[:, PAIRS : 2 * PAIRS]
+            margins = held.tile([P, COLUMNS], F32, name=f"margins{b}")
             step = PIECE // 2 if b == 0 else PAIRS // 2
-            for a in range(0, PAIRS, step):
-                pairs = slice(a, a + step)
-                nc.vector.tensor_tensor(differences[:, pairs], sides[:, 0, pairs], sides[:, 1, pairs], SUBTRACT)
-                if b == 0:
-                    nc.vector.tensor_scalar_mul(negatives[:, pairs], differences[:, pairs], -1.0)
-                else:
+            if b == 0:
+                in_order = margins[:].rearrange("p (a two) -> p a two", two=2)
+                by_pairs = raw[b][:].rearrange("p (a two) -> p a two", two=2)
+                for a in range(0, PAIRS, step):
+                    pairs = slice(a, a + step)
+                    nc.vector.tensor_tensor(in_order[:, pairs, :], by_pairs[:, pairs, :], by_pairs[:, pairs, ::-1], SUBTRACT)
+            else:
+                sides = raw[b][:].rearrange("p (a two) -> p two a", two=2)
+                differences = margins[:, 0:PAIRS]
+                negatives = margins[:, PAIRS : 2 * PAIRS]
+                for a in range(0, PAIRS, step):
+                    pairs = slice(a, a + step)
+                    nc.vector.tensor_tensor(differences[:, pairs], sides[:, 0, pairs], sides[:, 1, pairs], SUBTRACT)
                     nc.scalar.mul(negatives[:, pairs], differences[:, pairs], -1.0)
-            in_order = margins[:].rearrange("p (two a) -> p a two", two=2)
+                in_order = margins[:].rearrange("p (two a) -> p a two", two=2)
             for p_tile in (window[b], own[b]):
                 p_pairs = p_tile[:].rearrange("p (a two) -> p a two", two=2)
                 for a in range(0, PAIRS, step):

@@ -18,6 +18,17 @@ PIECE = 256
 FLOPS = 2 * RECORDS * COLUMNS
 
 
+def cut(total, width):
+    return [(start, width) for start in range(0, total, width)]
+
+
+def growing(total, first):
+    pieces = [(0, first)]
+    while sum(pieces[-1]) < total:
+        pieces.append((sum(pieces[-1]), sum(pieces[-1])))
+    return pieces
+
+
 def tile_rap_kernel(tc, logits, offs, out):
     nc = tc.nc
     with (
@@ -46,6 +57,7 @@ def tile_rap_kernel(tc, logits, offs, out):
 
         window = [held.tile([P, COLUMNS], F32, name=f"window{b}") for b in range(BLOCKS)]
         own = [held.tile([P, COLUMNS], F32, name=f"own{b}") for b in range(BLOCKS)]
+        own_pieces = {}
         for b in range(BLOCKS):
             margins = held.tile([P, COLUMNS], F32, name=f"margins{b}")
             step = PIECE // 2 if b == 0 else PAIRS // 2
@@ -64,10 +76,11 @@ def tile_rap_kernel(tc, logits, offs, out):
                     nc.vector.tensor_tensor(differences[:, pairs], sides[:, 0, pairs], sides[:, 1, pairs], SUBTRACT)
                     nc.scalar.mul(negatives[:, pairs], differences[:, pairs], -1.0)
                 in_order = margins[:].rearrange("p (two a) -> p a two", two=2)
-            for p_tile in (window[b], own[b]):
+            own_pieces[b] = growing(COLUMNS, PIECE // 2) if b == 0 else cut(COLUMNS, 2 * step)
+            for p_tile, pieces in ((window[b], cut(COLUMNS, 2 * step)), (own[b], own_pieces[b])):
                 p_pairs = p_tile[:].rearrange("p (a two) -> p a two", two=2)
-                for a in range(0, PAIRS, step):
-                    pairs = slice(a, a + step)
+                for j, width in pieces:
+                    pairs = slice(j // 2, (j + width) // 2)
                     nc.scalar.activation(p_pairs[:, pairs, :], in_order[:, pairs, :], SIGMOID)
 
         starts = range(0, COLUMNS, PIECE)
@@ -76,9 +89,13 @@ def tile_rap_kernel(tc, logits, offs, out):
             product = own[b]
             for k in range(LOOKUPS):
                 longer = held.tile([P, COLUMNS], F32, name=f"product{b}_{k}")
-                at_an_end = (b, k) in ((0, 0), (BLOCKS - 1, LOOKUPS - 1))
-                width = PIECE if at_an_end else 2 * PIECE
-                for j in range(0, COLUMNS, width):
+                if k == 0:
+                    pieces = own_pieces[b]
+                elif b == BLOCKS - 1:
+                    pieces = cut(COLUMNS, PIECE)
+                else:
+                    pieces = cut(COLUMNS, 2 * PIECE)
+                for j, width in pieces:
                     first = (k * COLUMNS + j) // 16
                     picked = window[b][:].indirect(offsets[:, first : first + width // 16])
                     nc.vector.tensor_tensor(longer[:, j : j + width], picked, product[:, j : j + width], MULT)

@@ -15,6 +15,9 @@ PAIRS = COLUMNS // 2
 LOOKUPS = 2
 PIECE = 256
 
+ROWS = 16
+ROW = COLUMNS // ROWS
+
 FLOPS = 2 * RECORDS * COLUMNS
 
 
@@ -47,8 +50,9 @@ def tile_rap_kernel(tc, logits, offs, out):
             for j in range(0, COLUMNS, COLUMNS // 2):
                 nc.sync.dma_start(raw[b][:, j : j + COLUMNS // 2], logits[b * P : (b + 1) * P, j : j + COLUMNS // 2])
 
-        averager = held.tile([P, 1], BF16, name="averager")
-        nc.vector.memset(averager[:], 1.0 / RECORDS)
+        averagers = held.tile([P, ROWS * ROWS], BF16, name="averagers")
+        nc.vector.memset(averagers[:], 0.0)
+        nc.vector.memset(averagers[:, :: ROWS + 1], 1.0 / RECORDS)
 
         scratch = held.tile([P, 1], F32, name="scratch")
         nc.vector.memset(scratch[:], 0.0)
@@ -83,8 +87,8 @@ def tile_rap_kernel(tc, logits, offs, out):
                     pairs = slice(j // 2, (j + width) // 2)
                     nc.scalar.activation(p_pairs[:, pairs, :], in_order[:, pairs, :], SIGMOID)
 
-        starts = range(0, COLUMNS, PIECE)
-        sums = [psum.tile([1, PIECE], F32, name=f"sums{j}") for j in starts]
+        last_pieces = cut(COLUMNS - PIECE, PIECE) + [(COLUMNS - PIECE, PIECE // 2), (COLUMNS - PIECE // 2, PIECE // 2)]
+        sums = psum.tile([ROWS, ROW], F32, name="sums")
         for b in range(BLOCKS):
             product = own[b]
             for k in range(LOOKUPS):
@@ -92,7 +96,7 @@ def tile_rap_kernel(tc, logits, offs, out):
                 if k == 0:
                     pieces = own_pieces[b]
                 elif b == BLOCKS - 1:
-                    pieces = cut(COLUMNS, PIECE)
+                    pieces = last_pieces
                 else:
                     pieces = cut(COLUMNS, 2 * PIECE)
                 for j, width in pieces:
@@ -102,17 +106,20 @@ def tile_rap_kernel(tc, logits, offs, out):
                 product = longer
 
             rounded = held.tile([P, COLUMNS], BF16, name=f"rounded{b}")
-            for bank, j in zip(sums, starts):
-                if b == BLOCKS - 1 and j == starts[-1]:
-                    nc.vector.tensor_copy(rounded[:, j : j + PIECE], product[:, j : j + PIECE])
+            for j, width in last_pieces if b == BLOCKS - 1 else cut(COLUMNS, PIECE):
+                if b == BLOCKS - 1 and j + width == COLUMNS:
+                    nc.vector.tensor_copy(rounded[:, j : j + width], product[:, j : j + width])
                 else:
-                    nc.scalar.copy(rounded[:, j : j + PIECE], product[:, j : j + PIECE])
-                nc.tensor.matmul(bank[:], averager[:], rounded[:, j : j + PIECE], start=(b == 0), stop=(b == BLOCKS - 1))
+                    nc.scalar.copy(rounded[:, j : j + width], product[:, j : j + width])
+                for r in range(j // ROW, (j + width) // ROW):
+                    nc.tensor.matmul(
+                        sums[:],
+                        averagers[:, r * ROWS : (r + 1) * ROWS],
+                        rounded[:, r * ROW : (r + 1) * ROW],
+                        start=(b == 0 and r == 0),
+                        stop=(b == BLOCKS - 1 and r == ROWS - 1),
+                    )
 
-        answers = held.tile([1, COLUMNS], F32, name="answers")
-        for bank, j in zip(sums, starts):
-            if j == starts[-1]:
-                nc.vector.tensor_copy(answers[:, j : j + PIECE], bank[:])
-            else:
-                nc.scalar.copy(answers[:, j : j + PIECE], bank[:])
-            nc.sync.dma_start(out[:, j : j + PIECE], answers[:, j : j + PIECE])
+        answers = held.tile([ROWS, ROW], F32, name="answers")
+        nc.vector.tensor_copy(answers[:], sums[:])
+        nc.sync.dma_start(out.rearrange("o (r n) -> (o r) n", r=ROWS), answers[:])

@@ -14,22 +14,23 @@ COLUMNS = 1024
 PAIRS = COLUMNS // 2
 LOOKUPS = 2
 PIECE = 256
-
+HALF = COLUMNS // 2
 ROWS = 16
 ROW = COLUMNS // ROWS
 
 FLOPS = 2 * RECORDS * COLUMNS
 
 
-def cut(total, width):
-    return [(start, width) for start in range(0, total, width)]
+def cut(start, end, width):
+    return [slice(j, j + width) for j in range(start, end, width)]
 
 
-def growing(total, first):
-    pieces = [(0, first)]
-    while sum(pieces[-1]) < total:
-        pieces.append((sum(pieces[-1]), sum(pieces[-1])))
-    return pieces
+def by_pairs(tile):
+    return tile[:].rearrange("p (a two) -> p a two", two=2)
+
+
+def pairs_of(columns):
+    return slice(columns.start // 2, columns.stop // 2)
 
 
 def tile_rap_kernel(tc, logits, offs, out):
@@ -39,16 +40,19 @@ def tile_rap_kernel(tc, logits, offs, out):
         tc.psum_pool(name="psum", bufs=1) as psum,
     ):
         offsets = held.tile([P, LOOKUPS * COLUMNS // 16], U16, name="offsets")
-
         raw = [held.tile([P, COLUMNS], F32, name=f"raw{b}") for b in range(BLOCKS)]
+        margins = [held.tile([P, COLUMNS], F32, name=f"margins{b}") for b in range(BLOCKS)]
+        window = [held.tile([P, COLUMNS], F32, name=f"window{b}") for b in range(BLOCKS)]
+        own = [held.tile([P, COLUMNS], F32, name=f"own{b}") for b in range(BLOCKS)]
+
+        pieces0 = cut(0, COLUMNS, PIECE)
         queues = (nc.sync, nc.scalar)
-        for j in range(0, COLUMNS, PIECE):
-            queue = queues[(j // PIECE) % len(queues)]
-            queue.dma_start(raw[0][:, j : j + PIECE], logits[0:P, j : j + PIECE])
+        for n, cols in enumerate(pieces0):
+            queues[n % len(queues)].dma_start(raw[0][:, cols], logits[0:P, cols])
         nc.sync.dma_start(offsets[:], offs)
-        for b in range(1, BLOCKS):
-            for j in range(0, COLUMNS, COLUMNS // 2):
-                nc.sync.dma_start(raw[b][:, j : j + COLUMNS // 2], logits[b * P : (b + 1) * P, j : j + COLUMNS // 2])
+        pieces1 = cut(0, COLUMNS, HALF)
+        for cols in pieces1:
+            nc.sync.dma_start(raw[1][:, cols], logits[P : 2 * P, cols])
 
         averagers = held.tile([P, ROWS * ROWS], BF16, name="averagers")
         nc.vector.memset(averagers[:], 0.0)
@@ -59,59 +63,55 @@ def tile_rap_kernel(tc, logits, offs, out):
         warmed = held.tile([P, 1], F32, name="warmed")
         nc.scalar.activation(warmed[:], scratch[:], SIGMOID)
 
-        window = [held.tile([P, COLUMNS], F32, name=f"window{b}") for b in range(BLOCKS)]
-        own = [held.tile([P, COLUMNS], F32, name=f"own{b}") for b in range(BLOCKS)]
-        own_pieces = {}
-        for b in range(BLOCKS):
-            margins = held.tile([P, COLUMNS], F32, name=f"margins{b}")
-            step = PIECE // 2 if b == 0 else PAIRS // 2
-            if b == 0:
-                in_order = margins[:].rearrange("p (a two) -> p a two", two=2)
-                by_pairs = raw[b][:].rearrange("p (a two) -> p a two", two=2)
-                for a in range(0, PAIRS, step):
-                    pairs = slice(a, a + step)
-                    nc.vector.tensor_tensor(in_order[:, pairs, :], by_pairs[:, pairs, :], by_pairs[:, pairs, ::-1], SUBTRACT)
-            else:
-                sides = raw[b][:].rearrange("p (a two) -> p two a", two=2)
-                differences = margins[:, 0:PAIRS]
-                negatives = margins[:, PAIRS : 2 * PAIRS]
-                for a in range(0, PAIRS, step):
-                    pairs = slice(a, a + step)
-                    nc.vector.tensor_tensor(differences[:, pairs], sides[:, 0, pairs], sides[:, 1, pairs], SUBTRACT)
-                    nc.scalar.mul(negatives[:, pairs], differences[:, pairs], -1.0)
-                in_order = margins[:].rearrange("p (two a) -> p a two", two=2)
-            own_pieces[b] = growing(COLUMNS, PIECE // 2) if b == 0 else cut(COLUMNS, 2 * step)
-            for p_tile, pieces in ((window[b], cut(COLUMNS, 2 * step)), (own[b], own_pieces[b])):
-                p_pairs = p_tile[:].rearrange("p (a two) -> p a two", two=2)
-                for j, width in pieces:
-                    pairs = slice(j // 2, (j + width) // 2)
-                    nc.scalar.activation(p_pairs[:, pairs, :], in_order[:, pairs, :], SIGMOID)
+        for cols in pieces0:
+            pairs = pairs_of(cols)
+            logit_pairs = by_pairs(raw[0])[:, pairs, :]
+            nc.vector.tensor_tensor(by_pairs(margins[0])[:, pairs, :], logit_pairs, logit_pairs[:, :, ::-1], SUBTRACT)
+        for cols in pieces0:
+            nc.scalar.activation(window[0][:, cols], margins[0][:, cols], SIGMOID)
+        copied = slice(0, HALF - PIECE // 2)
+        rest = slice(HALF - PIECE // 2, COLUMNS)
+        for cols in (slice(0, PIECE), slice(PIECE, copied.stop)):
+            nc.vector.tensor_copy(own[0][:, cols], window[0][:, cols])
+        nc.scalar.activation(own[0][:, rest], margins[0][:, rest], SIGMOID)
 
-        last_pieces = cut(COLUMNS - PIECE, PIECE) + [(COLUMNS - PIECE, PIECE // 2), (COLUMNS - PIECE // 2, PIECE // 2)]
+        differences = margins[1][:, 0:PAIRS]
+        negatives = margins[1][:, PAIRS:COLUMNS]
+        in_order = margins[1][:].rearrange("p (two a) -> p a two", two=2)
+        for cols in pieces1:
+            pairs = pairs_of(cols)
+            logit_pairs = by_pairs(raw[1])[:, pairs, :]
+            nc.vector.tensor_tensor(differences[:, pairs], logit_pairs[:, :, 0], logit_pairs[:, :, 1], SUBTRACT)
+            nc.scalar.mul(negatives[:, pairs], differences[:, pairs], -1.0)
+        for p_tile in (window[1], own[1]):
+            for cols in pieces1:
+                pairs = pairs_of(cols)
+                nc.scalar.activation(by_pairs(p_tile)[:, pairs, :], in_order[:, pairs, :], SIGMOID)
+
+        lookup_pieces = {
+            (0, 0): [copied, rest],
+            (0, 1): [copied, rest],
+            (1, 0): pieces1,
+            (1, 1): cut(0, COLUMNS - PIECE, PIECE) + cut(COLUMNS - PIECE, COLUMNS, PIECE // 2),
+        }
         sums = psum.tile([ROWS, ROW], F32, name="sums")
         for b in range(BLOCKS):
             product = own[b]
             for k in range(LOOKUPS):
                 longer = held.tile([P, COLUMNS], F32, name=f"product{b}_{k}")
-                if k == 0:
-                    pieces = own_pieces[b]
-                elif b == BLOCKS - 1:
-                    pieces = last_pieces
-                else:
-                    pieces = cut(COLUMNS, 2 * PIECE)
-                for j, width in pieces:
-                    first = (k * COLUMNS + j) // 16
-                    picked = window[b][:].indirect(offsets[:, first : first + width // 16])
-                    nc.vector.tensor_tensor(longer[:, j : j + width], picked, product[:, j : j + width], MULT)
+                for cols in lookup_pieces[b, k]:
+                    entries = slice((k * COLUMNS + cols.start) // 16, (k * COLUMNS + cols.stop) // 16)
+                    picked = window[b][:].indirect(offsets[:, entries])
+                    nc.vector.tensor_tensor(longer[:, cols], picked, product[:, cols], MULT)
                 product = longer
 
             rounded = held.tile([P, COLUMNS], BF16, name=f"rounded{b}")
-            for j, width in last_pieces if b == BLOCKS - 1 else cut(COLUMNS, PIECE):
-                if b == BLOCKS - 1 and j + width == COLUMNS:
-                    nc.vector.tensor_copy(rounded[:, j : j + width], product[:, j : j + width])
+            for cols in cut(0, COLUMNS, PIECE) if b == 0 else lookup_pieces[1, 1]:
+                if b == BLOCKS - 1 and cols.stop == COLUMNS:
+                    nc.vector.tensor_copy(rounded[:, cols], product[:, cols])
                 else:
-                    nc.scalar.copy(rounded[:, j : j + width], product[:, j : j + width])
-                for r in range(j // ROW, (j + width) // ROW):
+                    nc.scalar.copy(rounded[:, cols], product[:, cols])
+                for r in range(cols.start // ROW, cols.stop // ROW):
                     nc.tensor.matmul(
                         sums[:],
                         averagers[:, r * ROWS : (r + 1) * ROWS],

@@ -88,12 +88,14 @@ def tile_rap_kernel(tc, logits, offs, out):
                 pairs = pairs_of(cols)
                 nc.scalar.activation(by_pairs(p_tile)[:, pairs, :], in_order[:, pairs, :], SIGMOID)
 
+        last_small = [slice(COLUMNS - PIECE, COLUMNS - 2 * ROW), slice(COLUMNS - 2 * ROW, COLUMNS - ROW), slice(COLUMNS - ROW, COLUMNS)]
         lookup_pieces = {
             (0, 0): [copied, rest],
             (0, 1): [copied, rest],
             (1, 0): pieces1,
-            (1, 1): cut(0, COLUMNS - PIECE, PIECE) + cut(COLUMNS - PIECE, COLUMNS, PIECE // 2),
+            (1, 1): [slice(0, HALF), slice(HALF, COLUMNS - PIECE)] + last_small,
         }
+        rounding_pieces = [cut(0, COLUMNS, PIECE), cut(0, COLUMNS - PIECE, PIECE) + last_small]
         sums = psum.tile([ROWS, ROW], F32, name="sums")
         for b in range(BLOCKS):
             product = own[b]
@@ -106,7 +108,7 @@ def tile_rap_kernel(tc, logits, offs, out):
                 product = longer
 
             rounded = held.tile([P, COLUMNS], BF16, name=f"rounded{b}")
-            for cols in cut(0, COLUMNS, PIECE) if b == 0 else lookup_pieces[1, 1]:
+            for cols in rounding_pieces[b]:
                 if b == BLOCKS - 1 and cols.stop == COLUMNS:
                     nc.vector.tensor_copy(rounded[:, cols], product[:, cols])
                 else:

@@ -123,5 +123,5 @@ def tile_rap_kernel(tc, logits, offs, out):
                     )
 
         answers = held.tile([ROWS, ROW], F32, name="answers")
-        nc.vector.tensor_copy(answers[:], sums[:])
-        nc.sync.dma_start(out.rearrange("o (r n) -> (o r) n", r=ROWS), answers[:])
+        nc.scalar.copy(answers[:], sums[:])
+        nc.scalar.dma_start(out.rearrange("o (r n) -> (o r) n", r=ROWS), answers[:])

@@ -49,10 +49,10 @@ def tile_rap_kernel(tc, logits, offs, out):
         queues = (nc.sync, nc.scalar)
         for n, cols in enumerate(pieces0):
             queues[n % len(queues)].dma_start(raw[0][:, cols], logits[0:P, cols])
-        nc.sync.dma_start(offsets[:], offs)
         pieces1 = cut(0, COLUMNS, HALF)
-        for cols in pieces1:
-            nc.sync.dma_start(raw[1][:, cols], logits[P : 2 * P, cols])
+        nc.sync.dma_start(raw[1][:, pieces1[0]], logits[P : 2 * P, pieces1[0]])
+        nc.sync.dma_start(offsets[:], offs)
+        nc.sync.dma_start(raw[1][:, pieces1[1]], logits[P : 2 * P, pieces1[1]])
 
         averagers = held.tile([P, ROWS * ROWS], BF16, name="averagers")
         nc.vector.memset(averagers[:], 0.0)
@@ -63,11 +63,12 @@ def tile_rap_kernel(tc, logits, offs, out):
         warmed = held.tile([P, 1], F32, name="warmed")
         nc.scalar.activation(warmed[:], scratch[:], SIGMOID)
 
-        for cols in pieces0:
+        eighths = cut(0, COLUMNS, PIECE // 2)
+        for cols in eighths:
             pairs = pairs_of(cols)
             logit_pairs = by_pairs(raw[0])[:, pairs, :]
             nc.vector.tensor_tensor(by_pairs(margins[0])[:, pairs, :], logit_pairs, logit_pairs[:, :, ::-1], SUBTRACT)
-        for cols in pieces0:
+        for cols in eighths:
             nc.scalar.activation(window[0][:, cols], margins[0][:, cols], SIGMOID)
         copied = slice(0, HALF - PIECE // 2)
         rest = slice(HALF - PIECE // 2, COLUMNS)

@@ -49,7 +49,7 @@ def tile_rap_kernel(tc, logits, offs, out):
         queues = (nc.sync, nc.scalar)
         for n, cols in enumerate(pieces0):
             queues[n % len(queues)].dma_start(raw[0][:, cols], logits[0:P, cols])
-        pieces1 = cut(0, COLUMNS, HALF)
+        pieces1 = [slice(0, HALF + PIECE // 2), slice(HALF + PIECE // 2, COLUMNS)]
         nc.sync.dma_start(raw[1][:, pieces1[0]], logits[P : 2 * P, pieces1[0]])
         nc.sync.dma_start(offsets[:], offs)
         nc.sync.dma_start(raw[1][:, pieces1[1]], logits[P : 2 * P, pieces1[1]])

import concourse.mybir as mybir

F32 = mybir.dt.float32
BF16 = mybir.dt.bfloat16
U16 = mybir.dt.uint16
MULT = mybir.AluOpType.mult
SUBTRACT = mybir.AluOpType.subtract
SIGMOID = mybir.ActivationFunctionType.Sigmoid

P = 128
RECORDS = 256
BLOCKS = RECORDS // P
COLUMNS = 1024
PAIRS = COLUMNS // 2
LOOKUPS = 2
PIECE = 256
HALF = COLUMNS // 2
ROWS = 16
ROW = COLUMNS // ROWS

FLOPS = 2 * RECORDS * COLUMNS


def cut(start, end, width):
    return [slice(j, j + width) for j in range(start, end, width)]


def by_pairs(tile):
    return tile[:].rearrange("p (a two) -> p a two", two=2)


def pairs_of(columns):
    return slice(columns.start // 2, columns.stop // 2)


def tile_rap_kernel(tc, logits, offs, out):
    nc = tc.nc
    with (
        tc.tile_pool(name="held", bufs=1) as held,
        tc.psum_pool(name="psum", bufs=1) as psum,
    ):
        offsets = held.tile([P, LOOKUPS * COLUMNS // 16], U16, name="offsets")
        raw = [held.tile([P, COLUMNS], F32, name=f"raw{b}") for b in range(BLOCKS)]
        margins = [held.tile([P, COLUMNS], F32, name=f"margins{b}") for b in range(BLOCKS)]
        window = [held.tile([P, COLUMNS], F32, name=f"window{b}") for b in range(BLOCKS)]
        own = [held.tile([P, COLUMNS], F32, name=f"own{b}") for b in range(BLOCKS)]

        pieces0 = cut(0, COLUMNS, PIECE)
        queues = (nc.sync, nc.scalar)
        for n, cols in enumerate(pieces0):
            queues[n % len(queues)].dma_start(raw[0][:, cols], logits[0:P, cols])
        pieces1 = [slice(0, HALF + PIECE // 2), slice(HALF + PIECE // 2, COLUMNS)]
        nc.sync.dma_start(raw[1][:, pieces1[0]], logits[P : 2 * P, pieces1[0]])
        nc.sync.dma_start(offsets[:], offs)
        nc.sync.dma_start(raw[1][:, pieces1[1]], logits[P : 2 * P, pieces1[1]])

        averagers = held.tile([P, ROWS * ROWS], BF16, name="averagers")
        nc.vector.memset(averagers[:], 0.0)
        nc.vector.memset(averagers[:, :: ROWS + 1], 1.0 / RECORDS)

        scratch = held.tile([P, 1], F32, name="scratch")
        nc.vector.memset(scratch[:], 0.0)
        warmed = held.tile([P, 1], F32, name="warmed")
        nc.scalar.activation(warmed[:], scratch[:], SIGMOID)

        eighths = cut(0, COLUMNS, PIECE // 2)
        for cols in eighths:
            pairs = pairs_of(cols)
            logit_pairs = by_pairs(raw[0])[:, pairs, :]
            nc.vector.tensor_tensor(by_pairs(margins[0])[:, pairs, :], logit_pairs, logit_pairs[:, :, ::-1], SUBTRACT)
        for cols in eighths:
            nc.scalar.activation(window[0][:, cols], margins[0][:, cols], SIGMOID)
        copied = slice(0, HALF - PIECE // 2)
        rest = slice(HALF - PIECE // 2, COLUMNS)
        for cols in (slice(0, PIECE), slice(PIECE, copied.stop)):
            nc.vector.tensor_copy(own[0][:, cols], window[0][:, cols])
        nc.scalar.activation(own[0][:, rest], margins[0][:, rest], SIGMOID)

        differences = margins[1][:, 0:PAIRS]
        negatives = margins[1][:, PAIRS:COLUMNS]
        in_order = margins[1][:].rearrange("p (two a) -> p a two", two=2)
        for cols in pieces1:
            pairs = pairs_of(cols)
            logit_pairs = by_pairs(raw[1])[:, pairs, :]
            nc.vector.tensor_tensor(differences[:, pairs], logit_pairs[:, :, 0], logit_pairs[:, :, 1], SUBTRACT)
            nc.scalar.mul(negatives[:, pairs], differences[:, pairs], -1.0)
        for p_tile in (window[1], own[1]):
            for cols in pieces1:
                pairs = pairs_of(cols)
                nc.scalar.activation(by_pairs(p_tile)[:, pairs, :], in_order[:, pairs, :], SIGMOID)

        last_small = [slice(COLUMNS - PIECE, COLUMNS - 2 * ROW), slice(COLUMNS - 2 * ROW, COLUMNS - ROW), slice(COLUMNS - ROW, COLUMNS)]
        lookup_pieces = {
            (0, 0): [copied, rest],
            (0, 1): [copied, rest],
            (1, 0): pieces1,
            (1, 1): [slice(0, HALF), slice(HALF, COLUMNS - PIECE)] + last_small,
        }
        rounding_pieces = [cut(0, COLUMNS, PIECE), cut(0, COLUMNS - PIECE, PIECE) + last_small]
        sums = psum.tile([ROWS, ROW], F32, name="sums")
        for b in range(BLOCKS):
            product = own[b]
            for k in range(LOOKUPS):
                longer = held.tile([P, COLUMNS], F32, name=f"product{b}_{k}")
                for cols in lookup_pieces[b, k]:
                    entries = slice((k * COLUMNS + cols.start) // 16, (k * COLUMNS + cols.stop) // 16)
                    picked = window[b][:].indirect(offsets[:, entries])
                    nc.vector.tensor_tensor(longer[:, cols], picked, product[:, cols], MULT)
                product = longer

            rounded = held.tile([P, COLUMNS], BF16, name=f"rounded{b}")
            for cols in rounding_pieces[b]:
                if b == BLOCKS - 1 and cols.stop == COLUMNS:
                    nc.vector.tensor_copy(rounded[:, cols], product[:, cols])
                else:
                    nc.scalar.copy(rounded[:, cols], product[:, cols])
                for r in range(cols.start // ROW, cols.stop // ROW):
                    nc.tensor.matmul(
                        sums[:],
                        averagers[:, r * ROWS : (r + 1) * ROWS],
                        rounded[:, r * ROW : (r + 1) * ROW],
                        start=(b == 0 and r == 0),
                        stop=(b == BLOCKS - 1 and r == ROWS - 1),
                    )

        answers = held.tile([ROWS, ROW], F32, name="answers")
        nc.scalar.copy(answers[:], sums[:])
        nc.scalar.dma_start(out.rearrange("o (r n) -> (o r) n", r=ROWS), answers[:])
